import numpy as np
import ml_dtypes


def mxq(x, axis, fmt="e4m3"):
    dtype, down = {"e4m3": (ml_dtypes.float8_e4m3fn, 7), "e5m2": (ml_dtypes.float8_e5m2, 14)}[fmt]
    v = np.moveaxis(np.asarray(x, np.float32).astype(ml_dtypes.bfloat16).astype(np.float64), axis, -1)
    blocks = v.reshape(v.shape[:-1] + (-1, 32))
    amax = np.abs(blocks).max(-1, keepdims=True)
    byte = np.maximum(np.where(amax > 0, np.frexp(amax)[1] - 1 + 127, 0) - down, 1)
    scale = np.exp2(byte - 127.0)
    codes = (blocks / scale).astype(np.float32).astype(dtype).astype(np.float64)
    return np.moveaxis((codes * scale).reshape(v.shape), -1, axis)


WIDE = False


def mx_kscale(k):
    if not WIDE:
        return np.ones(k)
    levels = np.array([10, -10, 5, -5, 0])
    a = np.random.permutation(np.resize(levels, k // 512 * 4)).reshape(k // 512, 4)
    idx = np.arange(k)
    return np.exp2(a[idx // 512, idx % 128 // 32])


BF16 = ml_dtypes.bfloat16


def bf(x):
    return np.asarray(x, np.float32).astype(BF16)


def f64(x):
    return np.asarray(x).astype(np.float64)


E2M1 = np.array([0.0, 0.5, 1.0, 1.5, 2.0, 3.0, 4.0, 6.0, -0.0, -0.5, -1.0, -1.5, -2.0, -3.0, -4.0, -6.0])


def pack_weight(w, fmt):
    k, n = w.shape
    w = f64(bf(w)).reshape(k // 32, 32, n)
    amax = np.abs(w).max(1)
    if fmt == "e4m3":
        byte = np.frexp(amax)[1] - 1 + 127 - 7
    else:
        mant, ex = np.frexp(amax / 6.0)
        byte = np.where(mant > 0.5, ex, ex - 1) + 127
    byte = np.clip(np.where(amax > 0, byte, 1), 1, 254)
    scaled = (w * np.exp2(127.0 - byte)[:, None, :]).reshape(k, n).astype(np.float32)
    by_word = np.ascontiguousarray(scaled.reshape(k // 512, 128, 4, n).transpose(0, 1, 3, 2))
    if fmt == "e4m3":
        words = by_word.astype(ml_dtypes.float8_e4m3fn).view(np.uint8)
    else:
        c = by_word.astype(ml_dtypes.float4_e2m1fn).view(np.uint8) & 0xF
        words = c[..., 0::2] | (c[..., 1::2] << 4)
    return np.ascontiguousarray(words), np.ascontiguousarray(byte.astype(np.uint8).reshape(k // 512, 16, n))


def unpack_weight(words, scales, fmt):
    g, p, n, _ = words.shape
    if fmt == "e4m3":
        vals = np.ascontiguousarray(words).view(ml_dtypes.float8_e4m3fn).astype(np.float64)
    else:
        nib = np.empty((g, p, n, 4), np.uint8)
        nib[..., 0::2] = words & 0xF
        nib[..., 1::2] = words >> 4
        vals = E2M1[nib]
    vals = vals * np.repeat(np.exp2(scales.astype(np.float64) - 127.0), 8, axis=1)[..., None]
    return vals.transpose(0, 1, 3, 2).reshape(g * 512, n)


B, G0, G1, C0, C1, NC = 16, 8, 4, 512, 512, 58
NCH = 5 + 1 + NC
STRIDES = [8, 16]
SXY = [1.2, 1.1]
ANCH = [[[10, 13], [16, 30], [33, 23]], [[30, 61], [62, 45], [59, 119]]]
RAD = np.pi / 180.0
ANGLES = [RAD * a for a in (-60.0, -30.0, 0.0, 30.0, 60.0, 90.0)]
NA = len(ANCH[0]) * len(ANGLES)
FMT = "e4m3"


def sigmoid(v):
    return 1.0 / (1.0 + np.exp(-v))


def _masked_anchors(level):
    s = STRIDES[level]
    return np.array([[w / s, h / s, a] for (w, h) in ANCH[level] for a in ANGLES], dtype=np.float64)


def _decode(feat, W, b, level):
    Bn, C, G, _ = feat.shape
    out = (W @ mxq(feat.reshape(Bn, C, G * G), 1, "e4m3")) + b[None, :, None]
    pred = out.reshape(Bn, NA, NCH, G, G).transpose(0, 1, 3, 4, 2)
    sxy = SXY[level]
    s = float(STRIDES[level])
    ma = _masked_anchors(level)
    aw = ma[:, 0][None, :, None, None]
    ah = ma[:, 1][None, :, None, None]
    aa = ma[:, 2][None, :, None, None]
    gx = np.arange(G, dtype=np.float64)[None, None, None, :]
    gy = np.arange(G, dtype=np.float64)[None, None, :, None]
    px = sigmoid(pred[..., 0]) * sxy - (sxy - 1.0) / 2.0 + gx
    py = sigmoid(pred[..., 1]) * sxy - (sxy - 1.0) / 2.0 + gy
    pw = np.exp(pred[..., 2]) * aw
    ph = np.exp(pred[..., 3]) * ah
    pa = pred[..., 4] + aa
    conf = sigmoid(pred[..., 5])
    cls = sigmoid(pred[..., 6:])
    boxes = np.stack([px * s, py * s, pw * s, ph * s, pa], axis=-1)
    out = np.concatenate([boxes, conf[..., None], cls], axis=-1)
    return out.reshape(Bn, -1, NCH)


def _draw_level(G, C):
    s = mx_kscale(C)
    g = np.full(NCH, 1.5)
    g[2:4] = 0.3
    x = np.random.standard_normal((B, C, G, G)) * s[None, :, None, None]
    W = np.random.standard_normal((NA, NCH, C)) * g[None, :, None] / np.sqrt(C) / s
    b = np.random.standard_normal((NA, NCH)) * 0.4
    b[:, 2:4] -= 2.0
    words, scales = pack_weight(np.ascontiguousarray(W.reshape(NA * NCH, C).T), FMT)
    return bf(x), words, scales, bf(b.reshape(NA * NCH))


def setup_inputs():
    x0, W0_words, W0_scales, b0 = _draw_level(G0, C0)
    x1, W1_words, W1_scales, b1 = _draw_level(G1, C1)
    return {"x0": x0, "x1": x1, "W0_words": W0_words, "W0_scales": W0_scales, "b0": b0, "W1_words": W1_words, "W1_scales": W1_scales, "b1": b1}


def reference(x0, x1, W0_words, W0_scales, b0, W1_words, W1_scales, b1):
    o0 = _decode(f64(x0), unpack_weight(W0_words, W0_scales, FMT).T, f64(b0), 0)
    o1 = _decode(f64(x1), unpack_weight(W1_words, W1_scales, FMT).T, f64(b1), 1)
    return np.concatenate([o0, o1], axis=1)

@@ -1,0 +1,235 @@
+from contextlib import ExitStack
+
+import concourse.mybir as mybir
+
+F32 = mybir.dt.float32
+BF16 = mybir.dt.bfloat16
+I32 = mybir.dt.int32
+U8 = mybir.dt.uint8
+FP8X4 = mybir.dt.float8_e4m3fn_x4
+ACT = mybir.ActivationFunctionType
+ALU = mybir.AluOpType
+
+P = 128
+PACK = 4
+BATCH = 16
+ROWS = P // BATCH
+ANCHORS = 18
+ANGLE_DEGREES = (-60.0, -30.0, 0.0, 30.0, 60.0, 90.0)
+RADIANS_PER_DEGREE = 3.141592653589793 / 180.0
+FIELDS = 64
+OUT_CH = ANCHORS * FIELDS
+PAIR = 2
+BANK = 512
+BIAS_PAD = 1280
+QUANT_COLS = 2048
+
+LEVELS = (
+    dict(grid=8, grid_bits=3, stride=8.0, sxy=1.2, shapes=((10, 13), (16, 30), (33, 23)), first_row=0, pairs_per_store=1),
+    dict(grid=4, grid_bits=2, stride=16.0, sxy=1.1, shapes=((30, 61), (62, 45), (59, 119)), first_row=1152, pairs_per_store=3),
+)
+
+FLOPS = 2 * OUT_CH * 512 * BATCH * (8 * 8 + 4 * 4)
+
+
+def tile_detect_kernel(tc, x0, x1, W0_words, W0_scales, b0, W1_words, W1_scales, b1, out):
+    nc = tc.nc
+    inputs = ((x0, W0_words, W0_scales, b0), (x1, W1_words, W1_scales, b1))
+
+    with ExitStack() as stack:
+        keep = stack.enter_context(tc.tile_pool(name="keep", bufs=1))
+        psum = stack.enter_context(tc.psum_pool(name="psum", bufs=8))
+
+        ones = keep.tile([P, P], BF16)
+        nc.vector.memset(ones[:], 1.0)
+        bias_rows = keep.tile([P, 2, BIAS_PAD], BF16)
+        nc.vector.memset(bias_rows[:], 0.0)
+
+        tiles = [dict(), dict()]
+
+        def load(level):
+            x, w_words, w_scales, b = inputs[level]
+            t = tiles[level]
+            spots = LEVELS[level]["grid"] ** 2
+            nc.scalar.dma_start(out=bias_rows[0:1, level, 0:OUT_CH], in_=b.rearrange("(o n) -> o n", o=1))
+            x_raw = keep.tile([P, BATCH, PACK * spots], BF16, name="x_raw%d" % level)
+            x_view = x.rearrange("b (p t) h w -> p b (t h w)", t=PACK)
+            half = BATCH // 2
+            for b0_ in (0, half):
+                nc.sync.dma_start(out=x_raw[:, b0_ : b0_ + half, :], in_=x_view[:, b0_ : b0_ + half, :])
+            w_plane = keep.tile([P, OUT_CH], U8, name="w_plane%d" % level, align_bytes=64)
+            nc.vector.memset(w_plane[:].bitcast(I32), 0)
+            rows_by_r = w_scales[0].rearrange("(q r) n -> r q n", r=4)
+            for r in range(4):
+                nc.sync.dma_start(out=w_plane[r:P:32, :].bitcast(I32), in_=rows_by_r[r].bitcast(I32))
+            w_codes = keep.tile([P, OUT_CH], I32, name="w_codes%d" % level, align_bytes=64)
+            nc.sync.dma_start(out=w_codes[:], in_=w_words[0].rearrange("p n t -> p (n t)").bitcast(I32))
+            t["x_raw"], t["w_plane"], t["w_codes"] = x_raw, w_plane, w_codes
+
+        def constants(level):
+            lv = LEVELS[level]
+            t = tiles[level]
+            grid = lv["grid"]
+            groups = grid * grid // ROWS
+            sizes = keep.tile([P, ANCHORS, 2], F32, name="sizes%d" % level)
+            per_shape = len(ANGLE_DEGREES)
+            for i, wh in enumerate(lv["shapes"]):
+                for f in range(2):
+                    nc.gpsimd.memset(sizes[:, i * per_shape : (i + 1) * per_shape, f : f + 1], float(wh[f]))
+            spot = keep.tile([P, groups], I32, name="spot%d" % level)
+            nc.gpsimd.iota(spot[:], pattern=[[1, groups]], base=0, channel_multiplier=groups)
+            gx = keep.tile([P, groups], I32, name="gx%d" % level)
+            nc.vector.tensor_scalar(out=gx[:], in0=spot[:], scalar1=grid - 1, scalar2=None, op0=ALU.bitwise_and)
+            gy = keep.tile([P, groups], I32, name="gy%d" % level)
+            nc.vector.tensor_scalar(
+                out=gy[:], in0=spot[:], scalar1=grid * grid - 1, scalar2=lv["grid_bits"],
+                op0=ALU.bitwise_and, op1=ALU.logical_shift_right,
+            )
+            offsets = keep.tile([P, groups, 2], F32, name="offsets%d" % level)
+            shift = -(lv["sxy"] - 1.0) / 2.0
+            for f, g in enumerate((gx, gy)):
+                nc.vector.tensor_scalar(
+                    out=offsets[:, :, f : f + 1], in0=g[:].unsqueeze(2), scalar1=shift, scalar2=lv["stride"],
+                    op0=ALU.add, op1=ALU.mult,
+                )
+            t["sizes"], t["offsets"] = sizes, offsets
+
+        def spread_bias(level):
+            t = tiles[level]
+            bias = keep.tile([P, OUT_CH], F32, name="bias%d" % level)
+            for c0 in range(0, BIAS_PAD, BANK):
+                width = min(BANK, BIAS_PAD - c0)
+                used = min(width, OUT_CH - c0)
+                spread = psum.tile([P, BANK], F32, tag="bank")
+                nc.tensor.matmul(
+                    out=spread[:, 0:width], lhsT=ones[:], rhs=bias_rows[:, level, c0 : c0 + width], start=True, stop=True
+                )
+                nc.scalar.copy(out=bias[:, c0 : c0 + used], in_=spread[:, 0:used])
+            by_angle = bias[:].rearrange("p (i k f) -> p i k f", k=len(ANGLE_DEGREES), f=FIELDS)
+            for k, degrees in enumerate(ANGLE_DEGREES):
+                if degrees != 0.0:
+                    nc.gpsimd.tensor_scalar(
+                        out=by_angle[:, :, k, 4:5], in0=by_angle[:, :, k, 4:5], scalar1=RADIANS_PER_DEGREE * degrees,
+                        scalar2=None, op0=ALU.add,
+                    )
+            t["bias"] = bias
+
+        def quantise(level):
+            t = tiles[level]
+            groups = LEVELS[level]["grid"] ** 2 // ROWS
+            x_grouped = keep.tile([P, groups, P, PACK], BF16, name="x_grouped%d" % level, align_bytes=64)
+            dst = x_grouped[:].rearrange("p j (b r) t -> p j b r t", r=ROWS)
+            src = t["x_raw"][:].rearrange("p b (t r j) -> p j b r t", t=PACK, r=ROWS)
+            half = BATCH // 2
+            for b0_ in (0, half):
+                nc.vector.tensor_copy(out=dst[:, :, b0_ : b0_ + half], in_=src[:, :, b0_ : b0_ + half])
+            x_codes = keep.tile([P, groups * P], I32, name="x_codes%d" % level, align_bytes=64)
+            x_plane = keep.tile([P, groups * P], U8, name="x_plane%d" % level, align_bytes=64)
+            flat = x_grouped[:].rearrange("p j m t -> p (j m t)")
+            step = min(QUANT_COLS, groups * P * PACK) // PACK
+            for c0 in range(0, groups * P, step):
+                nc.vector.quantize_mx(
+                    out=x_codes[:, c0 : c0 + step].bitcast(FP8X4),
+                    scales=x_plane[:, c0 : c0 + step],
+                    in_=flat[:, PACK * c0 : PACK * (c0 + step)],
+                )
+            t["x_codes"], t["x_plane"] = x_codes, x_plane
+
+        def multiply(level, bank, j0, rhs, rhs_scale):
+            t = tiles[level]
+            for g in range(bank.shape[1]):
+                cols = slice((j0 + g) * P, (j0 + g + 1) * P)
+                nc.tensor.matmul_mx(
+                    out=bank[:, g, :],
+                    lhsT=t["x_codes"][:, cols].bitcast(FP8X4),
+                    lhsT_scale=t["x_plane"][:, cols],
+                    rhs=rhs.bitcast(FP8X4),
+                    rhs_scale=rhs_scale,
+                    start=True,
+                    stop=True,
+                )
+
+        def box_sizes(level):
+            t = tiles[level]
+            groups = LEVELS[level]["grid"] ** 2 // ROWS
+            in_bank = min(groups, BANK // P)
+            few_codes = keep.tile([P, P], I32, name="few_codes%d" % level, align_bytes=64)
+            few_plane = keep.tile([P, P], U8, name="few_plane%d" % level, align_bytes=64)
+            nc.vector.memset(few_codes[:], 0)
+            nc.vector.memset(few_plane[:].bitcast(I32), 0)
+            nc.vector.tensor_copy(
+                out=few_codes[:, 0 : ANCHORS * 4].rearrange("p (a f) -> p a f", f=4),
+                in_=t["w_codes"][:].rearrange("p (a f) -> p a f", f=FIELDS)[:, :, 0:4],
+            )
+            nc.vector.tensor_copy(
+                out=few_plane[:].bitcast(I32)[:, 0:ANCHORS].unsqueeze(2),
+                in_=t["w_plane"][:].bitcast(I32).rearrange("p (a g) -> p a g", g=FIELDS // 4)[:, :, 0:1],
+            )
+            wh = keep.tile([P, groups, ANCHORS, 2], F32, name="wh%d" % level)
+            bias_wh = t["bias"][:].rearrange("p (a f) -> p a f", f=FIELDS)[:, :, 2:4]
+            for j0 in range(0, groups, in_bank):
+                bank = psum.tile([P, in_bank, P], F32, tag="bank")
+                multiply(level, bank, j0, few_codes[:], few_plane[:])
+                nc.vector.tensor_tensor(
+                    out=wh[:, j0 : j0 + in_bank],
+                    in0=bank[:, :, 0 : ANCHORS * 4].rearrange("p g (a f) -> p g a f", f=4)[:, :, :, 2:4],
+                    in1=bias_wh.unsqueeze(1).to_broadcast([P, in_bank, ANCHORS, 2]),
+                    op=ALU.add,
+                )
+            nc.scalar.activation(out=wh[:], in_=wh[:], func=ACT.Exp)
+            nc.gpsimd.tensor_tensor(
+                out=wh[:], in0=wh[:], in1=t["sizes"][:].unsqueeze(1).to_broadcast([P, groups, ANCHORS, 2]), op=ALU.mult
+            )
+            t["wh"] = wh
+
+        def decode(level):
+            lv = LEVELS[level]
+            t = tiles[level]
+            spots = lv["grid"] ** 2
+            groups = spots // ROWS
+            in_bank = min(groups, BANK // P)
+            res = keep.tile([P, ANCHORS, groups, FIELDS], F32, name="res%d" % level)
+            step = PAIR * lv["pairs_per_store"]
+            for a0 in range(0, ANCHORS, step):
+                for a in range(a0, a0 + step, PAIR):
+                    cols = slice(a * FIELDS, (a + PAIR) * FIELDS)
+                    bias_pair = t["bias"][:, cols].rearrange("p (a f) -> p a f", f=FIELDS)
+                    for j0 in range(0, groups, in_bank):
+                        bank = psum.tile([P, in_bank, P], F32, tag="bank")
+                        multiply(level, bank, j0, t["w_codes"][:, cols], t["w_plane"][:, cols])
+                        nc.vector.tensor_tensor(
+                            out=res[:, a : a + PAIR, j0 : j0 + in_bank, :].rearrange("p a g f -> p g a f"),
+                            in0=bank[:].rearrange("p g (a f) -> p g a f", f=FIELDS),
+                            in1=bias_pair.unsqueeze(1).to_broadcast([P, in_bank, PAIR, FIELDS]),
+                            op=ALU.add,
+                        )
+                part = res[:, a0 : a0 + step]
+                nc.scalar.activation(out=part[:, :, :, 5:FIELDS], in_=part[:, :, :, 5:FIELDS], func=ACT.Sigmoid)
+                nc.scalar.copy(out=part[:, :, :, 2:4], in_=t["wh"][:, :, a0 : a0 + step, :].rearrange("p g a f -> p a g f"))
+                nc.scalar.activation(out=part[:, :, :, 0:2], in_=part[:, :, :, 0:2], func=ACT.Sigmoid)
+                nc.vector.scalar_tensor_tensor(
+                    out=part[:, :, :, 0:2],
+                    in0=part[:, :, :, 0:2],
+                    scalar=lv["sxy"] * lv["stride"],
+                    in1=t["offsets"][:].unsqueeze(1).to_broadcast([P, step, groups, 2]),
+                    op0=ALU.mult,
+                    op1=ALU.add,
+                )
+                for a in range(a0, a0 + step):
+                    row = lv["first_row"] + a * spots
+                    nc.sync.dma_start(
+                        out=out[:, row : row + spots, :].rearrange("b (r j) f -> b r (j f)", r=ROWS),
+                        in_=res[:, a].rearrange("p j f -> p (j f)"),
+                    )
+
+        order = (1, 0)
+        for level in order:
+            load(level)
+        for level in order:
+            constants(level)
+        for level in order:
+            spread_bias(level)
+            quantise(level)
+        for level in order:
+            box_sizes(level)
+            decode(level)

@@ -1,3 +1,4 @@
+import math
 from contextlib import ExitStack
 
 import concourse.mybir as mybir
@@ -18,15 +19,17 @@ ANCHORS = 18
 ANGLE_DEGREES = (-60.0, -30.0, 0.0, 30.0, 60.0, 90.0)
 RADIANS_PER_DEGREE = 3.141592653589793 / 180.0
 FIELDS = 64
+HEAD = 8
 OUT_CH = ANCHORS * FIELDS
 PAIR = 2
 BANK = 512
 BIAS_PAD = 1280
 QUANT_COLS = 2048
+LAG = 2
 
 LEVELS = (
-    dict(grid=8, grid_bits=3, stride=8.0, sxy=1.2, shapes=((10, 13), (16, 30), (33, 23)), first_row=0, pairs_per_store=1),
-    dict(grid=4, grid_bits=2, stride=16.0, sxy=1.1, shapes=((30, 61), (62, 45), (59, 119)), first_row=1152, pairs_per_store=3),
+    dict(grid=8, grid_bits=3, stride=8.0, sxy=1.2, shapes=((10, 13), (16, 30), (33, 23)), first_row=0, pairs=1),
+    dict(grid=4, grid_bits=2, stride=16.0, sxy=1.1, shapes=((30, 61), (62, 45), (59, 119)), first_row=1152, pairs=3),
 )
 
 FLOPS = 2 * OUT_CH * 512 * BATCH * (8 * 8 + 4 * 4)
@@ -35,47 +38,64 @@ FLOPS = 2 * OUT_CH * 512 * BATCH * (8 * 8 + 4 * 4)
 def tile_detect_kernel(tc, x0, x1, W0_words, W0_scales, b0, W1_words, W1_scales, b1, out):
     nc = tc.nc
     inputs = ((x0, W0_words, W0_scales, b0), (x1, W1_words, W1_scales, b1))
+    per_shape = len(ANGLE_DEGREES)
 
     with ExitStack() as stack:
+        stack.enter_context(tc.manual_schedule())
         keep = stack.enter_context(tc.tile_pool(name="keep", bufs=1))
         psum = stack.enter_context(tc.psum_pool(name="psum", bufs=8))
+        tiles = [dict(), dict()]
 
         ones = keep.tile([P, P], BF16)
         nc.vector.memset(ones[:], 1.0)
         bias_rows = keep.tile([P, 2, BIAS_PAD], BF16)
-        nc.vector.memset(bias_rows[:], 0.0)
+        nc.vector.memset(bias_rows[:].rearrange("p l n -> p (l n)").bitcast(I32), 0)
+        for level in (0, 1):
+            w_plane = keep.tile([P, OUT_CH], U8, name="w_plane%d" % level, align_bytes=64)
+            nc.vector.memset(w_plane[:].bitcast(I32), 0)
+            tiles[level]["w_plane"] = w_plane
 
-        tiles = [dict(), dict()]
-
-        def load(level):
-            x, w_words, w_scales, b = inputs[level]
-            t = tiles[level]
-            spots = LEVELS[level]["grid"] ** 2
+        for level in (0, 1):
+            b = inputs[level][3]
             nc.scalar.dma_start(out=bias_rows[0:1, level, 0:OUT_CH], in_=b.rearrange("(o n) -> o n", o=1))
+        for level in (0, 1):
+            x = inputs[level][0]
+            spots = LEVELS[level]["grid"] ** 2
             x_raw = keep.tile([P, BATCH, PACK * spots], BF16, name="x_raw%d" % level)
             x_view = x.rearrange("b (p t) h w -> p b (t h w)", t=PACK)
             half = BATCH // 2
-            for b0_ in (0, half):
-                nc.sync.dma_start(out=x_raw[:, b0_ : b0_ + half, :], in_=x_view[:, b0_ : b0_ + half, :])
-            w_plane = keep.tile([P, OUT_CH], U8, name="w_plane%d" % level, align_bytes=64)
-            nc.vector.memset(w_plane[:].bitcast(I32), 0)
+            for first in (0, half):
+                nc.sync.dma_start(out=x_raw[:, first : first + half, :], in_=x_view[:, first : first + half, :])
+            tiles[level]["x_raw"] = x_raw
+        for level in (0, 1):
+            w_words, w_scales = inputs[level][1], inputs[level][2]
+            w_plane = tiles[level]["w_plane"]
             rows_by_r = w_scales[0].rearrange("(q r) n -> r q n", r=4)
             for r in range(4):
                 nc.sync.dma_start(out=w_plane[r:P:32, :].bitcast(I32), in_=rows_by_r[r].bitcast(I32))
             w_codes = keep.tile([P, OUT_CH], I32, name="w_codes%d" % level, align_bytes=64)
             nc.sync.dma_start(out=w_codes[:], in_=w_words[0].rearrange("p n t -> p (n t)").bitcast(I32))
-            t["x_raw"], t["w_plane"], t["w_codes"] = x_raw, w_plane, w_codes
+            tiles[level]["w_codes"] = w_codes
 
-        def constants(level):
+        zero = keep.tile([P, per_shape], F32)
+        nc.vector.memset(zero[:], 0.0)
+        for level in (0, 1):
             lv = LEVELS[level]
-            t = tiles[level]
             grid = lv["grid"]
             groups = grid * grid // ROWS
-            sizes = keep.tile([P, ANCHORS, 2], F32, name="sizes%d" % level)
-            per_shape = len(ANGLE_DEGREES)
+            extra = keep.tile([P, ANCHORS, 3], F32, name="extra%d" % level)
             for i, wh in enumerate(lv["shapes"]):
                 for f in range(2):
-                    nc.gpsimd.memset(sizes[:, i * per_shape : (i + 1) * per_shape, f : f + 1], float(wh[f]))
+                    nc.vector.tensor_scalar(
+                        out=extra[:, i * per_shape : (i + 1) * per_shape, f : f + 1], in0=zero[:].unsqueeze(2),
+                        scalar1=math.log(wh[f]), scalar2=None, op0=ALU.add,
+                    )
+            by_angle = extra[:].rearrange("p (i k) f -> p i k f", k=per_shape)
+            for k, degrees in enumerate(ANGLE_DEGREES):
+                nc.vector.tensor_scalar(
+                    out=by_angle[:, :, k, 2:3], in0=zero[:, 0 : len(lv["shapes"])].unsqueeze(2),
+                    scalar1=RADIANS_PER_DEGREE * degrees, scalar2=None, op0=ALU.add,
+                )
             spot = keep.tile([P, groups], I32, name="spot%d" % level)
             nc.gpsimd.iota(spot[:], pattern=[[1, groups]], base=0, channel_multiplier=groups)
             gx = keep.tile([P, groups], I32, name="gx%d" % level)
@@ -85,17 +105,15 @@ def tile_detect_kernel(tc, x0, x1, W0_words, W0_scales, b0, W1_words, W1_scales,
                 out=gy[:], in0=spot[:], scalar1=grid * grid - 1, scalar2=lv["grid_bits"],
                 op0=ALU.bitwise_and, op1=ALU.logical_shift_right,
             )
-            offsets = keep.tile([P, groups, 2], F32, name="offsets%d" % level)
-            shift = -(lv["sxy"] - 1.0) / 2.0
+            centres = keep.tile([P, groups, 2], F32, name="centres%d" % level)
             for f, g in enumerate((gx, gy)):
                 nc.vector.tensor_scalar(
-                    out=offsets[:, :, f : f + 1], in0=g[:].unsqueeze(2), scalar1=shift, scalar2=lv["stride"],
+                    out=centres[:, :, f : f + 1], in0=g[:].unsqueeze(2), scalar1=0.5, scalar2=lv["stride"],
                     op0=ALU.add, op1=ALU.mult,
                 )
-            t["sizes"], t["offsets"] = sizes, offsets
+            tiles[level]["extra"], tiles[level]["centres"] = extra, centres
 
         def spread_bias(level):
-            t = tiles[level]
             bias = keep.tile([P, OUT_CH], F32, name="bias%d" % level)
             for c0 in range(0, BIAS_PAD, BANK):
                 width = min(BANK, BIAS_PAD - c0)
@@ -105,14 +123,7 @@ def tile_detect_kernel(tc, x0, x1, W0_words, W0_scales, b0, W1_words, W1_scales,
                     out=spread[:, 0:width], lhsT=ones[:], rhs=bias_rows[:, level, c0 : c0 + width], start=True, stop=True
                 )
                 nc.scalar.copy(out=bias[:, c0 : c0 + used], in_=spread[:, 0:used])
-            by_angle = bias[:].rearrange("p (i k f) -> p i k f", k=len(ANGLE_DEGREES), f=FIELDS)
-            for k, degrees in enumerate(ANGLE_DEGREES):
-                if degrees != 0.0:
-                    nc.gpsimd.tensor_scalar(
-                        out=by_angle[:, :, k, 4:5], in0=by_angle[:, :, k, 4:5], scalar1=RADIANS_PER_DEGREE * degrees,
-                        scalar2=None, op0=ALU.add,
-                    )
-            t["bias"] = bias
+            tiles[level]["bias"] = bias
 
         def quantise(level):
             t = tiles[level]
@@ -121,8 +132,8 @@ def tile_detect_kernel(tc, x0, x1, W0_words, W0_scales, b0, W1_words, W1_scales,
             dst = x_grouped[:].rearrange("p j (b r) t -> p j b r t", r=ROWS)
             src = t["x_raw"][:].rearrange("p b (t r j) -> p j b r t", t=PACK, r=ROWS)
             half = BATCH // 2
-            for b0_ in (0, half):
-                nc.vector.tensor_copy(out=dst[:, :, b0_ : b0_ + half], in_=src[:, :, b0_ : b0_ + half])
+            for first in (0, half):
+                nc.vector.tensor_copy(out=dst[:, :, first : first + half], in_=src[:, :, first : first + half])
             x_codes = keep.tile([P, groups * P], I32, name="x_codes%d" % level, align_bytes=64)
             x_plane = keep.tile([P, groups * P], U8, name="x_plane%d" % level, align_bytes=64)
             flat = x_grouped[:].rearrange("p j m t -> p (j m t)")
@@ -134,102 +145,81 @@ def tile_detect_kernel(tc, x0, x1, W0_words, W0_scales, b0, W1_words, W1_scales,
                     in_=flat[:, PACK * c0 : PACK * (c0 + step)],
                 )
             t["x_codes"], t["x_plane"] = x_codes, x_plane
+            by_field = t["bias"][:].rearrange("p (a f) -> p a f", f=FIELDS)
+            nc.vector.tensor_tensor(out=by_field[:, :, 2:5], in0=by_field[:, :, 2:5], in1=t["extra"][:], op=ALU.add)
+            t["res"] = keep.tile([P, ANCHORS, groups, FIELDS], F32, name="res%d" % level)
 
-        def multiply(level, bank, j0, rhs, rhs_scale):
-            t = tiles[level]
-            for g in range(bank.shape[1]):
-                cols = slice((j0 + g) * P, (j0 + g + 1) * P)
-                nc.tensor.matmul_mx(
-                    out=bank[:, g, :],
-                    lhsT=t["x_codes"][:, cols].bitcast(FP8X4),
-                    lhsT_scale=t["x_plane"][:, cols],
-                    rhs=rhs.bitcast(FP8X4),
-                    rhs_scale=rhs_scale,
-                    start=True,
-                    stop=True,
-                )
-
-        def box_sizes(level):
+        def logits(level, a0, step):
             t = tiles[level]
             groups = LEVELS[level]["grid"] ** 2 // ROWS
             in_bank = min(groups, BANK // P)
-            few_codes = keep.tile([P, P], I32, name="few_codes%d" % level, align_bytes=64)
-            few_plane = keep.tile([P, P], U8, name="few_plane%d" % level, align_bytes=64)
-            nc.vector.memset(few_codes[:], 0)
-            nc.vector.memset(few_plane[:].bitcast(I32), 0)
-            nc.vector.tensor_copy(
-                out=few_codes[:, 0 : ANCHORS * 4].rearrange("p (a f) -> p a f", f=4),
-                in_=t["w_codes"][:].rearrange("p (a f) -> p a f", f=FIELDS)[:, :, 0:4],
-            )
-            nc.vector.tensor_copy(
-                out=few_plane[:].bitcast(I32)[:, 0:ANCHORS].unsqueeze(2),
-                in_=t["w_plane"][:].bitcast(I32).rearrange("p (a g) -> p a g", g=FIELDS // 4)[:, :, 0:1],
-            )
-            wh = keep.tile([P, groups, ANCHORS, 2], F32, name="wh%d" % level)
-            bias_wh = t["bias"][:].rearrange("p (a f) -> p a f", f=FIELDS)[:, :, 2:4]
-            for j0 in range(0, groups, in_bank):
-                bank = psum.tile([P, in_bank, P], F32, tag="bank")
-                multiply(level, bank, j0, few_codes[:], few_plane[:])
-                nc.vector.tensor_tensor(
-                    out=wh[:, j0 : j0 + in_bank],
-                    in0=bank[:, :, 0 : ANCHORS * 4].rearrange("p g (a f) -> p g a f", f=4)[:, :, :, 2:4],
-                    in1=bias_wh.unsqueeze(1).to_broadcast([P, in_bank, ANCHORS, 2]),
-                    op=ALU.add,
-                )
-            nc.scalar.activation(out=wh[:], in_=wh[:], func=ACT.Exp)
-            nc.gpsimd.tensor_tensor(
-                out=wh[:], in0=wh[:], in1=t["sizes"][:].unsqueeze(1).to_broadcast([P, groups, ANCHORS, 2]), op=ALU.mult
-            )
-            t["wh"] = wh
+            for a in range(a0, a0 + step, PAIR):
+                cols = slice(a * FIELDS, (a + PAIR) * FIELDS)
+                bias_pair = t["bias"][:, cols].rearrange("p (a f) -> p a f", f=FIELDS)
+                for j0 in range(0, groups, in_bank):
+                    bank = psum.tile([P, in_bank, P], F32, tag="bank")
+                    for g in range(in_bank):
+                        spots = slice((j0 + g) * P, (j0 + g + 1) * P)
+                        nc.tensor.matmul_mx(
+                            out=bank[:, g, :],
+                            lhsT=t["x_codes"][:, spots].bitcast(FP8X4),
+                            lhsT_scale=t["x_plane"][:, spots],
+                            rhs=t["w_codes"][:, cols].bitcast(FP8X4),
+                            rhs_scale=t["w_plane"][:, cols],
+                            start=True,
+                            stop=True,
+                        )
+                    nc.vector.tensor_tensor(
+                        out=t["res"][:, a : a + PAIR, j0 : j0 + in_bank, :].rearrange("p a g f -> p g a f"),
+                        in0=bank[:].rearrange("p g (a f) -> p g a f", f=FIELDS),
+                        in1=bias_pair.unsqueeze(1).to_broadcast([P, in_bank, PAIR, FIELDS]),
+                        op=ALU.add,
+                    )
 
-        def decode(level):
+        def activate(level, a0, step):
+            part = tiles[level]["res"][:, a0 : a0 + step]
+            nc.scalar.activation(out=part[:, :, :, 5:FIELDS], in_=part[:, :, :, 5:FIELDS], func=ACT.Tanh, scale=0.5)
+            nc.gpsimd.tensor_scalar(
+                out=part[:, :, :, HEAD:FIELDS], in0=part[:, :, :, HEAD:FIELDS], scalar1=0.5, scalar2=0.5,
+                op0=ALU.mult, op1=ALU.add,
+            )
+            nc.scalar.activation(out=part[:, :, :, 5:HEAD], in_=part[:, :, :, 5:HEAD], func=ACT.Identity, scale=0.5, bias=0.5)
+            nc.scalar.activation(out=part[:, :, :, 2:4], in_=part[:, :, :, 2:4], func=ACT.Exp)
+            nc.scalar.activation(out=part[:, :, :, 0:2], in_=part[:, :, :, 0:2], func=ACT.Tanh, scale=0.5)
+
+        def finish(level, a0, step):
             lv = LEVELS[level]
             t = tiles[level]
             spots = lv["grid"] ** 2
             groups = spots // ROWS
-            in_bank = min(groups, BANK // P)
-            res = keep.tile([P, ANCHORS, groups, FIELDS], F32, name="res%d" % level)
-            step = PAIR * lv["pairs_per_store"]
-            for a0 in range(0, ANCHORS, step):
-                for a in range(a0, a0 + step, PAIR):
-                    cols = slice(a * FIELDS, (a + PAIR) * FIELDS)
-                    bias_pair = t["bias"][:, cols].rearrange("p (a f) -> p a f", f=FIELDS)
-                    for j0 in range(0, groups, in_bank):
-                        bank = psum.tile([P, in_bank, P], F32, tag="bank")
-                        multiply(level, bank, j0, t["w_codes"][:, cols], t["w_plane"][:, cols])
-                        nc.vector.tensor_tensor(
-                            out=res[:, a : a + PAIR, j0 : j0 + in_bank, :].rearrange("p a g f -> p g a f"),
-                            in0=bank[:].rearrange("p g (a f) -> p g a f", f=FIELDS),
-                            in1=bias_pair.unsqueeze(1).to_broadcast([P, in_bank, PAIR, FIELDS]),
-                            op=ALU.add,
-                        )
-                part = res[:, a0 : a0 + step]
-                nc.scalar.activation(out=part[:, :, :, 5:FIELDS], in_=part[:, :, :, 5:FIELDS], func=ACT.Sigmoid)
-                nc.scalar.copy(out=part[:, :, :, 2:4], in_=t["wh"][:, :, a0 : a0 + step, :].rearrange("p g a f -> p a g f"))
-                nc.scalar.activation(out=part[:, :, :, 0:2], in_=part[:, :, :, 0:2], func=ACT.Sigmoid)
-                nc.vector.scalar_tensor_tensor(
-                    out=part[:, :, :, 0:2],
-                    in0=part[:, :, :, 0:2],
-                    scalar=lv["sxy"] * lv["stride"],
-                    in1=t["offsets"][:].unsqueeze(1).to_broadcast([P, step, groups, 2]),
-                    op0=ALU.mult,
-                    op1=ALU.add,
+            part = t["res"][:, a0 : a0 + step]
+            nc.vector.scalar_tensor_tensor(
+                out=part[:, :, :, 0:2],
+                in0=part[:, :, :, 0:2],
+                scalar=lv["sxy"] * lv["stride"] / 2.0,
+                in1=t["centres"][:].unsqueeze(1).to_broadcast([P, step, groups, 2]),
+                op0=ALU.mult,
+                op1=ALU.add,
+            )
+            for a in range(a0, a0 + step):
+                row = lv["first_row"] + a * spots
+                nc.sync.dma_start(
+                    out=out[:, row : row + spots, :].rearrange("b (r j) f -> b r (j f)", r=ROWS),
+                    in_=t["res"][:, a].rearrange("p j f -> p (j f)"),
                 )
-                for a in range(a0, a0 + step):
-                    row = lv["first_row"] + a * spots
-                    nc.sync.dma_start(
-                        out=out[:, row : row + spots, :].rearrange("b (r j) f -> b r (j f)", r=ROWS),
-                        in_=res[:, a].rearrange("p j f -> p (j f)"),
-                    )
 
-        order = (1, 0)
-        for level in order:
-            load(level)
-        for level in order:
-            constants(level)
-        for level in order:
+        for level in (0, 1):
             spread_bias(level)
+        for level in (0, 1):
             quantise(level)
-        for level in order:
-            box_sizes(level)
-            decode(level)
+
+        chunks = []
+        for level in (0, 1):
+            step = PAIR * LEVELS[level]["pairs"]
+            chunks.extend((level, a0, step) for a0 in range(0, ANCHORS, step))
+        for i in range(len(chunks) + LAG):
+            if i < len(chunks):
+                logits(*chunks[i])
+                activate(*chunks[i])
+            if i >= LAG:
+                finish(*chunks[i - LAG])

@@ -25,11 +25,12 @@ PAIR = 2
 BANK = 512
 BIAS_PAD = 1280
 QUANT_COLS = 2048
+PREPARE_AT = 3
 LAG = 2
 
 LEVELS = (
-    dict(grid=8, grid_bits=3, stride=8.0, sxy=1.2, shapes=((10, 13), (16, 30), (33, 23)), first_row=0, pairs=1),
-    dict(grid=4, grid_bits=2, stride=16.0, sxy=1.1, shapes=((30, 61), (62, 45), (59, 119)), first_row=1152, pairs=3),
+    dict(grid=8, grid_bits=3, stride=8.0, sxy=1.2, shapes=((10, 13), (16, 30), (33, 23)), first_row=0, pairs=1, images_per_load=4),
+    dict(grid=4, grid_bits=2, stride=16.0, sxy=1.1, shapes=((30, 61), (62, 45), (59, 119)), first_row=1152, pairs=3, images_per_load=16),
 )
 
 FLOPS = 2 * OUT_CH * 512 * BATCH * (8 * 8 + 4 * 4)
@@ -59,16 +60,14 @@ def tile_detect_kernel(tc, x0, x1, W0_words, W0_scales, b0, W1_words, W1_scales,
             b = inputs[level][3]
             nc.scalar.dma_start(out=bias_rows[0:1, level, 0:OUT_CH], in_=b.rearrange("(o n) -> o n", o=1))
         for level in (0, 1):
-            x = inputs[level][0]
+            x, w_words, w_scales = inputs[level][0:3]
             spots = LEVELS[level]["grid"] ** 2
             x_raw = keep.tile([P, BATCH, PACK * spots], BF16, name="x_raw%d" % level)
             x_view = x.rearrange("b (p t) h w -> p b (t h w)", t=PACK)
-            half = BATCH // 2
-            for first in (0, half):
-                nc.sync.dma_start(out=x_raw[:, first : first + half, :], in_=x_view[:, first : first + half, :])
+            images = LEVELS[level]["images_per_load"]
+            for first in range(0, BATCH, images):
+                nc.sync.dma_start(out=x_raw[:, first : first + images, :], in_=x_view[:, first : first + images, :])
             tiles[level]["x_raw"] = x_raw
-        for level in (0, 1):
-            w_words, w_scales = inputs[level][1], inputs[level][2]
             w_plane = tiles[level]["w_plane"]
             rows_by_r = w_scales[0].rearrange("(q r) n -> r q n", r=4)
             for r in range(4):
@@ -131,9 +130,9 @@ def tile_detect_kernel(tc, x0, x1, W0_words, W0_scales, b0, W1_words, W1_scales,
             x_grouped = keep.tile([P, groups, P, PACK], BF16, name="x_grouped%d" % level, align_bytes=64)
             dst = x_grouped[:].rearrange("p j (b r) t -> p j b r t", r=ROWS)
             src = t["x_raw"][:].rearrange("p b (t r j) -> p j b r t", t=PACK, r=ROWS)
-            half = BATCH // 2
-            for first in (0, half):
-                nc.vector.tensor_copy(out=dst[:, :, first : first + half], in_=src[:, :, first : first + half])
+            images = LEVELS[level]["images_per_load"]
+            for first in range(0, BATCH, images):
+                nc.vector.tensor_copy(out=dst[:, :, first : first + images], in_=src[:, :, first : first + images])
             x_codes = keep.tile([P, groups * P], I32, name="x_codes%d" % level, align_bytes=64)
             x_plane = keep.tile([P, groups * P], U8, name="x_plane%d" % level, align_bytes=64)
             flat = x_grouped[:].rearrange("p j m t -> p (j m t)")
@@ -183,8 +182,8 @@ def tile_detect_kernel(tc, x0, x1, W0_words, W0_scales, b0, W1_words, W1_scales,
                 out=part[:, :, :, HEAD:FIELDS], in0=part[:, :, :, HEAD:FIELDS], scalar1=0.5, scalar2=0.5,
                 op0=ALU.mult, op1=ALU.add,
             )
-            nc.scalar.activation(out=part[:, :, :, 5:HEAD], in_=part[:, :, :, 5:HEAD], func=ACT.Identity, scale=0.5, bias=0.5)
             nc.scalar.activation(out=part[:, :, :, 2:4], in_=part[:, :, :, 2:4], func=ACT.Exp)
+            nc.scalar.activation(out=part[:, :, :, 5:HEAD], in_=part[:, :, :, 5:HEAD], func=ACT.Identity, scale=0.5, bias=0.5)
             nc.scalar.activation(out=part[:, :, :, 0:2], in_=part[:, :, :, 0:2], func=ACT.Tanh, scale=0.5)
 
         def finish(level, a0, step):
@@ -210,8 +209,7 @@ def tile_detect_kernel(tc, x0, x1, W0_words, W0_scales, b0, W1_words, W1_scales,
 
         for level in (0, 1):
             spread_bias(level)
-        for level in (0, 1):
-            quantise(level)
+        quantise(0)
 
         chunks = []
         for level in (0, 1):
@@ -221,5 +219,7 @@ def tile_detect_kernel(tc, x0, x1, W0_words, W0_scales, b0, W1_words, W1_scales,
             if i < len(chunks):
                 logits(*chunks[i])
                 activate(*chunks[i])
+            if i == PREPARE_AT:
+                quantise(1)
             if i >= LAG:
                 finish(*chunks[i - LAG])

@@ -97,6 +97,13 @@ def tile_detect_kernel(tc, x0, x1, W0_words, W0_scales, b0, W1_words, W1_scales,
                 )
             spot = keep.tile([P, groups], I32, name="spot%d" % level)
             nc.gpsimd.iota(spot[:], pattern=[[1, groups]], base=0, channel_multiplier=groups)
+            tiles[level]["extra"], tiles[level]["spot"] = extra, spot
+
+        def cell_centres(level):
+            lv = LEVELS[level]
+            grid = lv["grid"]
+            groups = grid * grid // ROWS
+            spot = tiles[level]["spot"]
             gx = keep.tile([P, groups], I32, name="gx%d" % level)
             nc.vector.tensor_scalar(out=gx[:], in0=spot[:], scalar1=grid - 1, scalar2=None, op0=ALU.bitwise_and)
             gy = keep.tile([P, groups], I32, name="gy%d" % level)
@@ -110,7 +117,7 @@ def tile_detect_kernel(tc, x0, x1, W0_words, W0_scales, b0, W1_words, W1_scales,
                     out=centres[:, :, f : f + 1], in0=g[:].unsqueeze(2), scalar1=0.5, scalar2=lv["stride"],
                     op0=ALU.add, op1=ALU.mult,
                 )
-            tiles[level]["extra"], tiles[level]["centres"] = extra, centres
+            tiles[level]["centres"] = centres
 
         def spread_bias(level):
             bias = keep.tile([P, OUT_CH], F32, name="bias%d" % level)
@@ -128,11 +135,16 @@ def tile_detect_kernel(tc, x0, x1, W0_words, W0_scales, b0, W1_words, W1_scales,
             t = tiles[level]
             groups = LEVELS[level]["grid"] ** 2 // ROWS
             x_grouped = keep.tile([P, groups, P, PACK], BF16, name="x_grouped%d" % level, align_bytes=64)
-            dst = x_grouped[:].rearrange("p j (b r) t -> p j b r t", r=ROWS)
-            src = t["x_raw"][:].rearrange("p b (t r j) -> p j b r t", t=PACK, r=ROWS)
+            dst = x_grouped[:].rearrange("p j (b r) t -> p b r j t", r=ROWS)
+            src = t["x_raw"][:].rearrange("p b (t r j) -> p b r j t", t=PACK, r=ROWS)
             images = LEVELS[level]["images_per_load"]
+            few = min(groups, PACK)
             for first in range(0, BATCH, images):
-                nc.vector.tensor_copy(out=dst[:, :, first : first + images], in_=src[:, :, first : first + images])
+                for j0 in range(0, groups, few):
+                    nc.vector.tensor_copy(
+                        out=dst[:, first : first + images, :, j0 : j0 + few, :],
+                        in_=src[:, first : first + images, :, j0 : j0 + few, :],
+                    )
             x_codes = keep.tile([P, groups * P], I32, name="x_codes%d" % level, align_bytes=64)
             x_plane = keep.tile([P, groups * P], U8, name="x_plane%d" % level, align_bytes=64)
             flat = x_grouped[:].rearrange("p j m t -> p (j m t)")
@@ -210,6 +222,8 @@ def tile_detect_kernel(tc, x0, x1, W0_words, W0_scales, b0, W1_words, W1_scales,
         for level in (0, 1):
             spread_bias(level)
         quantise(0)
+        for level in (0, 1):
+            cell_centres(level)
 
         chunks = []
         for level in (0, 1):

@@ -26,6 +26,7 @@ BANK = 512
 BIAS_PAD = 1280
 QUANT_COLS = 2048
 PREPARE_AT = 3
+SMALL_LEVEL_AT = 5
 LAG = 2
 
 LEVELS = (
@@ -47,8 +48,12 @@ def tile_detect_kernel(tc, x0, x1, W0_words, W0_scales, b0, W1_words, W1_scales,
         psum = stack.enter_context(tc.psum_pool(name="psum", bufs=8))
         tiles = [dict(), dict()]
 
+        zero = keep.tile([P, per_shape], F32)
+        nc.gpsimd.memset(zero[:], 0.0)
+        warm = keep.tile([P, 1], F32)
+        nc.scalar.activation(out=warm[:], in_=zero[:, 0:1], func=ACT.Exp)
         ones = keep.tile([P, P], BF16)
-        nc.vector.memset(ones[:], 1.0)
+        nc.gpsimd.memset(ones[:], 1.0)
         bias_rows = keep.tile([P, 2, BIAS_PAD], BF16)
         nc.vector.memset(bias_rows[:].rearrange("p l n -> p (l n)").bitcast(I32), 0)
         for level in (0, 1):
@@ -76,28 +81,28 @@ def tile_detect_kernel(tc, x0, x1, W0_words, W0_scales, b0, W1_words, W1_scales,
             nc.sync.dma_start(out=w_codes[:], in_=w_words[0].rearrange("p n t -> p (n t)").bitcast(I32))
             tiles[level]["w_codes"] = w_codes
 
-        zero = keep.tile([P, per_shape], F32)
-        nc.vector.memset(zero[:], 0.0)
+        for level in (0, 1):
+            groups = LEVELS[level]["grid"] ** 2 // ROWS
+            spot = keep.tile([P, groups], I32, name="spot%d" % level)
+            nc.gpsimd.iota(spot[:], pattern=[[1, groups]], base=0, channel_multiplier=groups)
+            tiles[level]["spot"] = spot
+        angle_index = keep.tile([P, per_shape], F32)
+        nc.gpsimd.iota(angle_index[:], pattern=[[1, per_shape]], base=0, channel_multiplier=0, allow_small_or_imprecise_dtypes=True)
         for level in (0, 1):
             lv = LEVELS[level]
-            grid = lv["grid"]
-            groups = grid * grid // ROWS
             extra = keep.tile([P, ANCHORS, 3], F32, name="extra%d" % level)
             for i, wh in enumerate(lv["shapes"]):
                 for f in range(2):
-                    nc.vector.tensor_scalar(
+                    nc.gpsimd.tensor_scalar(
                         out=extra[:, i * per_shape : (i + 1) * per_shape, f : f + 1], in0=zero[:].unsqueeze(2),
-                        scalar1=math.log(wh[f]), scalar2=None, op0=ALU.add,
+                        scalar1=1.0, scalar2=math.log(wh[f]), op0=ALU.mult, op1=ALU.add,
                     )
-            by_angle = extra[:].rearrange("p (i k) f -> p i k f", k=per_shape)
-            for k, degrees in enumerate(ANGLE_DEGREES):
-                nc.vector.tensor_scalar(
-                    out=by_angle[:, :, k, 2:3], in0=zero[:, 0 : len(lv["shapes"])].unsqueeze(2),
-                    scalar1=RADIANS_PER_DEGREE * degrees, scalar2=None, op0=ALU.add,
+                nc.gpsimd.tensor_scalar(
+                    out=extra[:, i * per_shape : (i + 1) * per_shape, 2:3], in0=angle_index[:].unsqueeze(2),
+                    scalar1=RADIANS_PER_DEGREE * (ANGLE_DEGREES[1] - ANGLE_DEGREES[0]), scalar2=RADIANS_PER_DEGREE * ANGLE_DEGREES[0],
+                    op0=ALU.mult, op1=ALU.add,
                 )
-            spot = keep.tile([P, groups], I32, name="spot%d" % level)
-            nc.gpsimd.iota(spot[:], pattern=[[1, groups]], base=0, channel_multiplier=groups)
-            tiles[level]["extra"], tiles[level]["spot"] = extra, spot
+            tiles[level]["extra"] = extra
 
         def cell_centres(level):
             lv = LEVELS[level]
@@ -131,7 +136,10 @@ def tile_detect_kernel(tc, x0, x1, W0_words, W0_scales, b0, W1_words, W1_scales,
                 nc.scalar.copy(out=bias[:, c0 : c0 + used], in_=spread[:, 0:used])
             tiles[level]["bias"] = bias
 
-        def quantise(level):
+        def times_one(out, in_):
+            nc.gpsimd.tensor_scalar(out=out, in0=in_, scalar1=1.0, scalar2=0.0, op0=ALU.mult, op1=ALU.add)
+
+        def regroup(level, copy):
             t = tiles[level]
             groups = LEVELS[level]["grid"] ** 2 // ROWS
             x_grouped = keep.tile([P, groups, P, PACK], BF16, name="x_grouped%d" % level, align_bytes=64)
@@ -141,10 +149,16 @@ def tile_detect_kernel(tc, x0, x1, W0_words, W0_scales, b0, W1_words, W1_scales,
             few = min(groups, PACK)
             for first in range(0, BATCH, images):
                 for j0 in range(0, groups, few):
-                    nc.vector.tensor_copy(
+                    copy(
                         out=dst[:, first : first + images, :, j0 : j0 + few, :],
                         in_=src[:, first : first + images, :, j0 : j0 + few, :],
                     )
+            t["x_grouped"] = x_grouped
+
+        def quantise(level):
+            t = tiles[level]
+            groups = LEVELS[level]["grid"] ** 2 // ROWS
+            x_grouped = t["x_grouped"]
             x_codes = keep.tile([P, groups * P], I32, name="x_codes%d" % level, align_bytes=64)
             x_plane = keep.tile([P, groups * P], U8, name="x_plane%d" % level, align_bytes=64)
             flat = x_grouped[:].rearrange("p j m t -> p (j m t)")
@@ -195,7 +209,6 @@ def tile_detect_kernel(tc, x0, x1, W0_words, W0_scales, b0, W1_words, W1_scales,
                 op0=ALU.mult, op1=ALU.add,
             )
             nc.scalar.activation(out=part[:, :, :, 2:4], in_=part[:, :, :, 2:4], func=ACT.Exp)
-            nc.scalar.activation(out=part[:, :, :, 5:HEAD], in_=part[:, :, :, 5:HEAD], func=ACT.Identity, scale=0.5, bias=0.5)
             nc.scalar.activation(out=part[:, :, :, 0:2], in_=part[:, :, :, 0:2], func=ACT.Tanh, scale=0.5)
 
         def finish(level, a0, step):
@@ -204,6 +217,9 @@ def tile_detect_kernel(tc, x0, x1, W0_words, W0_scales, b0, W1_words, W1_scales,
             spots = lv["grid"] ** 2
             groups = spots // ROWS
             part = t["res"][:, a0 : a0 + step]
+            nc.vector.tensor_scalar(
+                out=part[:, :, :, 5:HEAD], in0=part[:, :, :, 5:HEAD], scalar1=0.5, scalar2=0.5, op0=ALU.mult, op1=ALU.add
+            )
             nc.vector.scalar_tensor_tensor(
                 out=part[:, :, :, 0:2],
                 in0=part[:, :, :, 0:2],
@@ -221,14 +237,17 @@ def tile_detect_kernel(tc, x0, x1, W0_words, W0_scales, b0, W1_words, W1_scales,
 
         for level in (0, 1):
             spread_bias(level)
-        quantise(0)
-        for level in (0, 1):
             cell_centres(level)
+        regroup(1, times_one)
+        regroup(0, nc.vector.tensor_copy)
+        quantise(0)
 
         chunks = []
         for level in (0, 1):
             step = PAIR * LEVELS[level]["pairs"]
             chunks.extend((level, a0, step) for a0 in range(0, ANCHORS, step))
+        large = ANCHORS // PAIR
+        chunks = chunks[0:SMALL_LEVEL_AT] + chunks[large:] + chunks[SMALL_LEVEL_AT:large]
         for i in range(len(chunks) + LAG):
             if i < len(chunks):
                 logits(*chunks[i])

@@ -201,22 +201,26 @@ def tile_detect_kernel(tc, x0, x1, W0_words, W0_scales, b0, W1_words, W1_scales,
                         op=ALU.add,
                     )
 
-        def activate(level, a0, step):
+        def halve(engine, level, a0, step):
+            part = tiles[level]["res"][:, a0 : a0 + step, :, HEAD:FIELDS]
+            engine.tensor_scalar(out=part, in0=part, scalar1=0.5, scalar2=0.5, op0=ALU.mult, op1=ALU.add)
+
+        def activate(level, a0, step, is_last):
             part = tiles[level]["res"][:, a0 : a0 + step]
             nc.scalar.activation(out=part[:, :, :, 5:FIELDS], in_=part[:, :, :, 5:FIELDS], func=ACT.Tanh, scale=0.5)
-            nc.gpsimd.tensor_scalar(
-                out=part[:, :, :, HEAD:FIELDS], in0=part[:, :, :, HEAD:FIELDS], scalar1=0.5, scalar2=0.5,
-                op0=ALU.mult, op1=ALU.add,
-            )
+            if not is_last:
+                halve(nc.gpsimd, level, a0, step)
             nc.scalar.activation(out=part[:, :, :, 2:4], in_=part[:, :, :, 2:4], func=ACT.Exp)
             nc.scalar.activation(out=part[:, :, :, 0:2], in_=part[:, :, :, 0:2], func=ACT.Tanh, scale=0.5)
 
-        def finish(level, a0, step):
+        def finish(level, a0, step, is_last):
             lv = LEVELS[level]
             t = tiles[level]
             spots = lv["grid"] ** 2
             groups = spots // ROWS
             part = t["res"][:, a0 : a0 + step]
+            if is_last:
+                halve(nc.vector, level, a0, step)
             nc.vector.tensor_scalar(
                 out=part[:, :, :, 5:HEAD], in0=part[:, :, :, 5:HEAD], scalar1=0.5, scalar2=0.5, op0=ALU.mult, op1=ALU.add
             )
@@ -251,8 +255,8 @@ def tile_detect_kernel(tc, x0, x1, W0_words, W0_scales, b0, W1_words, W1_scales,
         for i in range(len(chunks) + LAG):
             if i < len(chunks):
                 logits(*chunks[i])
-                activate(*chunks[i])
+                activate(*chunks[i], i == len(chunks) - 1)
             if i == PREPARE_AT:
                 quantise(1)
             if i >= LAG:
-                finish(*chunks[i - LAG])
+                finish(*chunks[i - LAG], i - LAG == len(chunks) - 1)

@@ -23,7 +23,6 @@ HEAD = 8
 OUT_CH = ANCHORS * FIELDS
 PAIR = 2
 BANK = 512
-BIAS_PAD = 1280
 QUANT_COLS = 2048
 PREPARE_AT = 3
 SMALL_LEVEL_AT = 5
@@ -54,7 +53,7 @@ def tile_detect_kernel(tc, x0, x1, W0_words, W0_scales, b0, W1_words, W1_scales,
         nc.scalar.activation(out=warm[:], in_=zero[:, 0:1], func=ACT.Exp)
         ones = keep.tile([P, P], BF16)
         nc.gpsimd.memset(ones[:], 1.0)
-        bias_rows = keep.tile([P, 2, BIAS_PAD], BF16)
+        bias_rows = keep.tile([P, 2, OUT_CH], BF16)
         nc.vector.memset(bias_rows[:].rearrange("p l n -> p (l n)").bitcast(I32), 0)
         for level in (0, 1):
             w_plane = keep.tile([P, OUT_CH], U8, name="w_plane%d" % level, align_bytes=64)
@@ -126,14 +125,13 @@ def tile_detect_kernel(tc, x0, x1, W0_words, W0_scales, b0, W1_words, W1_scales,
 
         def spread_bias(level):
             bias = keep.tile([P, OUT_CH], F32, name="bias%d" % level)
-            for c0 in range(0, BIAS_PAD, BANK):
-                width = min(BANK, BIAS_PAD - c0)
-                used = min(width, OUT_CH - c0)
+            for c0 in range(0, OUT_CH, BANK):
+                width = min(BANK, OUT_CH - c0)
                 spread = psum.tile([P, BANK], F32, tag="bank")
                 nc.tensor.matmul(
                     out=spread[:, 0:width], lhsT=ones[:], rhs=bias_rows[:, level, c0 : c0 + width], start=True, stop=True
                 )
-                nc.scalar.copy(out=bias[:, c0 : c0 + used], in_=spread[:, 0:used])
+                nc.scalar.copy(out=bias[:, c0 : c0 + width], in_=spread[:, 0:width])
             tiles[level]["bias"] = bias
 
         def times_one(out, in_):

@@ -56,7 +56,7 @@ def tile_detect_kernel(tc, x0, x1, W0_words, W0_scales, b0, W1_words, W1_scales,
         bias_rows = keep.tile([P, 2, OUT_CH], BF16)
         nc.vector.memset(bias_rows[:].rearrange("p l n -> p (l n)").bitcast(I32), 0)
         for level in (0, 1):
-            w_plane = keep.tile([P, OUT_CH], U8, name="w_plane%d" % level, align_bytes=64)
+            w_plane = keep.tile([P, OUT_CH], U8, name="w_plane%d" % level, align_bytes=256)
             nc.vector.memset(w_plane[:].bitcast(I32), 0)
             tiles[level]["w_plane"] = w_plane
 
@@ -66,7 +66,7 @@ def tile_detect_kernel(tc, x0, x1, W0_words, W0_scales, b0, W1_words, W1_scales,
         for level in (0, 1):
             x, w_words, w_scales = inputs[level][0:3]
             spots = LEVELS[level]["grid"] ** 2
-            x_raw = keep.tile([P, BATCH, PACK * spots], BF16, name="x_raw%d" % level)
+            x_raw = keep.tile([P, BATCH, PACK * spots], BF16, name="x_raw%d" % level, align_bytes=256)
             x_view = x.rearrange("b (p t) h w -> p b (t h w)", t=PACK)
             images = LEVELS[level]["images_per_load"]
             for first in range(0, BATCH, images):
@@ -76,7 +76,7 @@ def tile_detect_kernel(tc, x0, x1, W0_words, W0_scales, b0, W1_words, W1_scales,
             rows_by_r = w_scales[0].rearrange("(q r) n -> r q n", r=4)
             for r in range(4):
                 nc.sync.dma_start(out=w_plane[r:P:32, :].bitcast(I32), in_=rows_by_r[r].bitcast(I32))
-            w_codes = keep.tile([P, OUT_CH], I32, name="w_codes%d" % level, align_bytes=64)
+            w_codes = keep.tile([P, OUT_CH], I32, name="w_codes%d" % level, align_bytes=256)
             nc.sync.dma_start(out=w_codes[:], in_=w_words[0].rearrange("p n t -> p (n t)").bitcast(I32))
             tiles[level]["w_codes"] = w_codes
 
@@ -124,7 +124,7 @@ def tile_detect_kernel(tc, x0, x1, W0_words, W0_scales, b0, W1_words, W1_scales,
             tiles[level]["centres"] = centres
 
         def spread_bias(level):
-            bias = keep.tile([P, OUT_CH], F32, name="bias%d" % level)
+            bias = keep.tile([P, OUT_CH], F32, name="bias%d" % level, align_bytes=256)
             for c0 in range(0, OUT_CH, BANK):
                 width = min(BANK, OUT_CH - c0)
                 spread = psum.tile([P, BANK], F32, tag="bank")
@@ -140,7 +140,7 @@ def tile_detect_kernel(tc, x0, x1, W0_words, W0_scales, b0, W1_words, W1_scales,
         def regroup(level, copy):
             t = tiles[level]
             groups = LEVELS[level]["grid"] ** 2 // ROWS
-            x_grouped = keep.tile([P, groups, P, PACK], BF16, name="x_grouped%d" % level, align_bytes=64)
+            x_grouped = keep.tile([P, groups, P, PACK], BF16, name="x_grouped%d" % level, align_bytes=256)
             dst = x_grouped[:].rearrange("p j (b r) t -> p b r j t", r=ROWS)
             src = t["x_raw"][:].rearrange("p b (t r j) -> p b r j t", t=PACK, r=ROWS)
             images = LEVELS[level]["images_per_load"]
@@ -157,8 +157,8 @@ def tile_detect_kernel(tc, x0, x1, W0_words, W0_scales, b0, W1_words, W1_scales,
             t = tiles[level]
             groups = LEVELS[level]["grid"] ** 2 // ROWS
             x_grouped = t["x_grouped"]
-            x_codes = keep.tile([P, groups * P], I32, name="x_codes%d" % level, align_bytes=64)
-            x_plane = keep.tile([P, groups * P], U8, name="x_plane%d" % level, align_bytes=64)
+            x_codes = keep.tile([P, groups * P], I32, name="x_codes%d" % level, align_bytes=256)
+            x_plane = keep.tile([P, groups * P], U8, name="x_plane%d" % level, align_bytes=256)
             flat = x_grouped[:].rearrange("p j m t -> p (j m t)")
             step = min(QUANT_COLS, groups * P * PACK) // PACK
             for c0 in range(0, groups * P, step):
@@ -170,7 +170,7 @@ def tile_detect_kernel(tc, x0, x1, W0_words, W0_scales, b0, W1_words, W1_scales,
             t["x_codes"], t["x_plane"] = x_codes, x_plane
             by_field = t["bias"][:].rearrange("p (a f) -> p a f", f=FIELDS)
             nc.vector.tensor_tensor(out=by_field[:, :, 2:5], in0=by_field[:, :, 2:5], in1=t["extra"][:], op=ALU.add)
-            t["res"] = keep.tile([P, ANCHORS, groups, FIELDS], F32, name="res%d" % level)
+            t["res"] = keep.tile([P, ANCHORS, groups, FIELDS], F32, name="res%d" % level, align_bytes=256)
 
         def logits(level, a0, step):
             t = tiles[level]

@@ -72,12 +72,13 @@ def tile_detect_kernel(tc, x0, x1, W0_words, W0_scales, b0, W1_words, W1_scales,
             for first in range(0, BATCH, images):
                 nc.sync.dma_start(out=x_raw[:, first : first + images, :], in_=x_view[:, first : first + images, :])
             tiles[level]["x_raw"] = x_raw
+            w_codes = keep.tile([P, OUT_CH], I32, name="w_codes%d" % level, align_bytes=256)
+            words = w_words[0].rearrange("p n t -> p (n t)").bitcast(I32)
             w_plane = tiles[level]["w_plane"]
             rows_by_r = w_scales[0].rearrange("(q r) n -> r q n", r=4)
             for r in range(4):
                 nc.sync.dma_start(out=w_plane[r:P:32, :].bitcast(I32), in_=rows_by_r[r].bitcast(I32))
-            w_codes = keep.tile([P, OUT_CH], I32, name="w_codes%d" % level, align_bytes=256)
-            nc.sync.dma_start(out=w_codes[:], in_=w_words[0].rearrange("p n t -> p (n t)").bitcast(I32))
+            nc.sync.dma_start(out=w_codes[:], in_=words)
             tiles[level]["w_codes"] = w_codes
 
         for level in (0, 1):
@@ -88,15 +89,14 @@ def tile_detect_kernel(tc, x0, x1, W0_words, W0_scales, b0, W1_words, W1_scales,
         angle_index = keep.tile([P, per_shape], F32)
         nc.gpsimd.iota(angle_index[:], pattern=[[1, per_shape]], base=0, channel_multiplier=0, allow_small_or_imprecise_dtypes=True)
         for level in (0, 1):
-            lv = LEVELS[level]
             extra = keep.tile([P, ANCHORS, 3], F32, name="extra%d" % level)
-            for i, wh in enumerate(lv["shapes"]):
+            for i, wh in enumerate(LEVELS[level]["shapes"]):
                 for f in range(2):
-                    nc.gpsimd.tensor_scalar(
+                    nc.vector.tensor_scalar(
                         out=extra[:, i * per_shape : (i + 1) * per_shape, f : f + 1], in0=zero[:].unsqueeze(2),
                         scalar1=1.0, scalar2=math.log(wh[f]), op0=ALU.mult, op1=ALU.add,
                     )
-                nc.gpsimd.tensor_scalar(
+                nc.vector.tensor_scalar(
                     out=extra[:, i * per_shape : (i + 1) * per_shape, 2:3], in0=angle_index[:].unsqueeze(2),
                     scalar1=RADIANS_PER_DEGREE * (ANGLE_DEGREES[1] - ANGLE_DEGREES[0]), scalar2=RADIANS_PER_DEGREE * ANGLE_DEGREES[0],
                     op0=ALU.mult, op1=ALU.add,
@@ -199,29 +199,24 @@ def tile_detect_kernel(tc, x0, x1, W0_words, W0_scales, b0, W1_words, W1_scales,
                         op=ALU.add,
                     )
 
-        def halve(engine, level, a0, step):
-            part = tiles[level]["res"][:, a0 : a0 + step, :, HEAD:FIELDS]
+        def halve(engine, level, a0, step, first, last):
+            part = tiles[level]["res"][:, a0 : a0 + step, :, first:last]
             engine.tensor_scalar(out=part, in0=part, scalar1=0.5, scalar2=0.5, op0=ALU.mult, op1=ALU.add)
 
-        def activate(level, a0, step, is_last):
+        def activate_boxes(level, a0, step):
             part = tiles[level]["res"][:, a0 : a0 + step]
-            nc.scalar.activation(out=part[:, :, :, 5:FIELDS], in_=part[:, :, :, 5:FIELDS], func=ACT.Tanh, scale=0.5)
-            if not is_last:
-                halve(nc.gpsimd, level, a0, step)
             nc.scalar.activation(out=part[:, :, :, 2:4], in_=part[:, :, :, 2:4], func=ACT.Exp)
             nc.scalar.activation(out=part[:, :, :, 0:2], in_=part[:, :, :, 0:2], func=ACT.Tanh, scale=0.5)
 
-        def finish(level, a0, step, is_last):
+        def activate_sigmoids(level, a0, step):
+            part = tiles[level]["res"][:, a0 : a0 + step, :, 5:FIELDS]
+            nc.scalar.activation(out=part, in_=part, func=ACT.Tanh, scale=0.5)
+
+        def finish_boxes(level, a0, step):
             lv = LEVELS[level]
             t = tiles[level]
-            spots = lv["grid"] ** 2
-            groups = spots // ROWS
+            groups = lv["grid"] ** 2 // ROWS
             part = t["res"][:, a0 : a0 + step]
-            if is_last:
-                halve(nc.vector, level, a0, step)
-            nc.vector.tensor_scalar(
-                out=part[:, :, :, 5:HEAD], in0=part[:, :, :, 5:HEAD], scalar1=0.5, scalar2=0.5, op0=ALU.mult, op1=ALU.add
-            )
             nc.vector.scalar_tensor_tensor(
                 out=part[:, :, :, 0:2],
                 in0=part[:, :, :, 0:2],
@@ -230,6 +225,11 @@ def tile_detect_kernel(tc, x0, x1, W0_words, W0_scales, b0, W1_words, W1_scales,
                 op0=ALU.mult,
                 op1=ALU.add,
             )
+
+        def store(level, a0, step):
+            lv = LEVELS[level]
+            t = tiles[level]
+            spots = lv["grid"] ** 2
             for a in range(a0, a0 + step):
                 row = lv["first_row"] + a * spots
                 nc.sync.dma_start(
@@ -250,11 +250,29 @@ def tile_detect_kernel(tc, x0, x1, W0_words, W0_scales, b0, W1_words, W1_scales,
             chunks.extend((level, a0, step) for a0 in range(0, ANCHORS, step))
         large = ANCHORS // PAIR
         chunks = chunks[0:SMALL_LEVEL_AT] + chunks[large:] + chunks[SMALL_LEVEL_AT:large]
-        for i in range(len(chunks) + LAG):
-            if i < len(chunks):
-                logits(*chunks[i])
-                activate(*chunks[i], i == len(chunks) - 1)
+
+        def finish(level, a0, step):
+            halve(nc.vector, level, a0, step, 5, HEAD)
+            finish_boxes(level, a0, step)
+            store(level, a0, step)
+
+        last = len(chunks) - 1
+        for i, chunk in enumerate(chunks):
+            logits(*chunk)
+            if i < last:
+                activate_sigmoids(*chunk)
+                halve(nc.gpsimd, *chunk, HEAD, FIELDS)
+                activate_boxes(*chunk)
             if i == PREPARE_AT:
                 quantise(1)
             if i >= LAG:
-                finish(*chunks[i - LAG], i - LAG == len(chunks) - 1)
+                finish(*chunks[i - LAG])
+        finish(*chunks[last - 1])
+        level, a0, step = chunks[last]
+        activate_boxes(level, a0, step)
+        for a in range(a0, a0 + step):
+            activate_sigmoids(level, a, 1)
+        finish_boxes(level, a0, step)
+        for a in range(a0, a0 + step):
+            halve(nc.vector, level, a, 1, 5, FIELDS)
+            store(level, a, 1)

@@ -49,8 +49,6 @@ def tile_detect_kernel(tc, x0, x1, W0_words, W0_scales, b0, W1_words, W1_scales,
 
         zero = keep.tile([P, per_shape], F32)
         nc.gpsimd.memset(zero[:], 0.0)
-        warm = keep.tile([P, 1], F32)
-        nc.scalar.activation(out=warm[:], in_=zero[:, 0:1], func=ACT.Exp)
         ones = keep.tile([P, P], BF16)
         nc.gpsimd.memset(ones[:], 1.0)
         bias_rows = keep.tile([P, 2, OUT_CH], BF16)
@@ -61,9 +59,6 @@ def tile_detect_kernel(tc, x0, x1, W0_words, W0_scales, b0, W1_words, W1_scales,
             tiles[level]["w_plane"] = w_plane
 
         for level in (0, 1):
-            b = inputs[level][3]
-            nc.scalar.dma_start(out=bias_rows[0:1, level, 0:OUT_CH], in_=b.rearrange("(o n) -> o n", o=1))
-        for level in (0, 1):
             x, w_words, w_scales = inputs[level][0:3]
             spots = LEVELS[level]["grid"] ** 2
             x_raw = keep.tile([P, BATCH, PACK * spots], BF16, name="x_raw%d" % level, align_bytes=256)
@@ -72,14 +67,22 @@ def tile_detect_kernel(tc, x0, x1, W0_words, W0_scales, b0, W1_words, W1_scales,
             for first in range(0, BATCH, images):
                 nc.sync.dma_start(out=x_raw[:, first : first + images, :], in_=x_view[:, first : first + images, :])
             tiles[level]["x_raw"] = x_raw
+            if level == 0:
+                for bias_level in (0, 1):
+                    b = inputs[bias_level][3]
+                    nc.scalar.dma_start(out=bias_rows[0:1, bias_level, 0:OUT_CH], in_=b.rearrange("(o n) -> o n", o=1))
             w_codes = keep.tile([P, OUT_CH], I32, name="w_codes%d" % level, align_bytes=256)
             words = w_words[0].rearrange("p n t -> p (n t)").bitcast(I32)
             w_plane = tiles[level]["w_plane"]
             rows_by_r = w_scales[0].rearrange("(q r) n -> r q n", r=4)
             for r in range(4):
                 nc.sync.dma_start(out=w_plane[r:P:32, :].bitcast(I32), in_=rows_by_r[r].bitcast(I32))
-            nc.sync.dma_start(out=w_codes[:], in_=words)
+                if r == 0:
+                    nc.sync.dma_start(out=w_codes[:], in_=words)
             tiles[level]["w_codes"] = w_codes
+
+        warm = keep.tile([P, 1], F32)
+        nc.scalar.activation(out=warm[:], in_=zero[:, 0:1], func=ACT.Exp)
 
         for level in (0, 1):
             groups = LEVELS[level]["grid"] ** 2 // ROWS

@@ -23,6 +23,7 @@ HEAD = 8
 OUT_CH = ANCHORS * FIELDS
 PAIR = 2
 BANK = 512
+FIRST_ANCHORS = BANK // FIELDS
 QUANT_COLS = 2048
 PREPARE_AT = 3
 SMALL_LEVEL_AT = 5
@@ -156,6 +157,11 @@ def tile_detect_kernel(tc, x0, x1, W0_words, W0_scales, b0, W1_words, W1_scales,
                     )
             t["x_grouped"] = x_grouped
 
+        def shift_bias(engine, level, a0, a1):
+            t = tiles[level]
+            part = t["bias"][:].rearrange("p (a f) -> p a f", f=FIELDS)[:, a0:a1, 2:5]
+            engine.tensor_tensor(out=part, in0=part, in1=t["extra"][:, a0:a1], op=ALU.add)
+
         def quantise(level):
             t = tiles[level]
             groups = LEVELS[level]["grid"] ** 2 // ROWS
@@ -170,9 +176,9 @@ def tile_detect_kernel(tc, x0, x1, W0_words, W0_scales, b0, W1_words, W1_scales,
                     scales=x_plane[:, c0 : c0 + step],
                     in_=flat[:, PACK * c0 : PACK * (c0 + step)],
                 )
+                if level == 0 and c0 == 0:
+                    shift_bias(nc.vector, 0, 0, FIRST_ANCHORS)
             t["x_codes"], t["x_plane"] = x_codes, x_plane
-            by_field = t["bias"][:].rearrange("p (a f) -> p a f", f=FIELDS)
-            nc.vector.tensor_tensor(out=by_field[:, :, 2:5], in0=by_field[:, :, 2:5], in1=t["extra"][:], op=ALU.add)
             t["res"] = keep.tile([P, ANCHORS, groups, FIELDS], F32, name="res%d" % level, align_bytes=256)
 
         def logits(level, a0, step):
@@ -244,6 +250,7 @@ def tile_detect_kernel(tc, x0, x1, W0_words, W0_scales, b0, W1_words, W1_scales,
             spread_bias(level)
             cell_centres(level)
         regroup(1, times_one)
+        shift_bias(nc.gpsimd, 1, 0, ANCHORS)
         regroup(0, nc.vector.tensor_copy)
         quantise(0)
 
@@ -262,6 +269,8 @@ def tile_detect_kernel(tc, x0, x1, W0_words, W0_scales, b0, W1_words, W1_scales,
         last = len(chunks) - 1
         for i, chunk in enumerate(chunks):
             logits(*chunk)
+            if i == 0:
+                shift_bias(nc.vector, 0, FIRST_ANCHORS, ANCHORS)
             if i < last:
                 activate_sigmoids(*chunk)
                 halve(nc.gpsimd, *chunk, HEAD, FIELDS)

import math
from contextlib import ExitStack

import concourse.mybir as mybir

F32 = mybir.dt.float32
BF16 = mybir.dt.bfloat16
I32 = mybir.dt.int32
U8 = mybir.dt.uint8
FP8X4 = mybir.dt.float8_e4m3fn_x4
ACT = mybir.ActivationFunctionType
ALU = mybir.AluOpType

P = 128
PACK = 4
BATCH = 16
ROWS = P // BATCH
ANCHORS = 18
ANGLE_DEGREES = (-60.0, -30.0, 0.0, 30.0, 60.0, 90.0)
RADIANS_PER_DEGREE = 3.141592653589793 / 180.0
FIELDS = 64
HEAD = 8
OUT_CH = ANCHORS * FIELDS
PAIR = 2
BANK = 512
FIRST_ANCHORS = BANK // FIELDS
QUANT_COLS = 2048
PREPARE_AT = 3
SMALL_LEVEL_AT = 5
LAG = 2

LEVELS = (
    dict(grid=8, grid_bits=3, stride=8.0, sxy=1.2, shapes=((10, 13), (16, 30), (33, 23)), first_row=0, pairs=1, images_per_load=4),
    dict(grid=4, grid_bits=2, stride=16.0, sxy=1.1, shapes=((30, 61), (62, 45), (59, 119)), first_row=1152, pairs=3, images_per_load=16),
)

FLOPS = 2 * OUT_CH * 512 * BATCH * (8 * 8 + 4 * 4)


def tile_detect_kernel(tc, x0, x1, W0_words, W0_scales, b0, W1_words, W1_scales, b1, out):
    nc = tc.nc
    inputs = ((x0, W0_words, W0_scales, b0), (x1, W1_words, W1_scales, b1))
    per_shape = len(ANGLE_DEGREES)

    with ExitStack() as stack:
        stack.enter_context(tc.manual_schedule())
        keep = stack.enter_context(tc.tile_pool(name="keep", bufs=1))
        psum = stack.enter_context(tc.psum_pool(name="psum", bufs=8))
        tiles = [dict(), dict()]

        zero = keep.tile([P, per_shape], F32)
        nc.gpsimd.memset(zero[:], 0.0)
        ones = keep.tile([P, P], BF16)
        nc.gpsimd.memset(ones[:], 1.0)
        bias_rows = keep.tile([P, 2, OUT_CH], BF16)
        nc.vector.memset(bias_rows[:].rearrange("p l n -> p (l n)").bitcast(I32), 0)
        for level in (0, 1):
            w_plane = keep.tile([P, OUT_CH], U8, name="w_plane%d" % level, align_bytes=256)
            nc.vector.memset(w_plane[:].bitcast(I32), 0)
            tiles[level]["w_plane"] = w_plane

        for level in (0, 1):
            x, w_words, w_scales = inputs[level][0:3]
            spots = LEVELS[level]["grid"] ** 2
            x_raw = keep.tile([P, BATCH, PACK * spots], BF16, name="x_raw%d" % level, align_bytes=256)
            x_view = x.rearrange("b (p t) h w -> p b (t h w)", t=PACK)
            images = LEVELS[level]["images_per_load"]
            for first in range(0, BATCH, images):
                nc.sync.dma_start(out=x_raw[:, first : first + images, :], in_=x_view[:, first : first + images, :])
            tiles[level]["x_raw"] = x_raw
            if level == 0:
                for bias_level in (0, 1):
                    b = inputs[bias_level][3]
                    nc.scalar.dma_start(out=bias_rows[0:1, bias_level, 0:OUT_CH], in_=b.rearrange("(o n) -> o n", o=1))
            w_codes = keep.tile([P, OUT_CH], I32, name="w_codes%d" % level, align_bytes=256)
            words = w_words[0].rearrange("p n t -> p (n t)").bitcast(I32)
            w_plane = tiles[level]["w_plane"]
            rows_by_r = w_scales[0].rearrange("(q r) n -> r q n", r=4)
            for r in range(4):
                nc.sync.dma_start(out=w_plane[r:P:32, :].bitcast(I32), in_=rows_by_r[r].bitcast(I32))
                if r == 0:
                    nc.sync.dma_start(out=w_codes[:], in_=words)
            tiles[level]["w_codes"] = w_codes

        warm = keep.tile([P, 1], F32)
        nc.scalar.activation(out=warm[:], in_=zero[:, 0:1], func=ACT.Exp)

        for level in (0, 1):
            groups = LEVELS[level]["grid"] ** 2 // ROWS
            spot = keep.tile([P, groups], I32, name="spot%d" % level)
            nc.gpsimd.iota(spot[:], pattern=[[1, groups]], base=0, channel_multiplier=groups)
            tiles[level]["spot"] = spot
        angle_index = keep.tile([P, per_shape], F32)
        nc.gpsimd.iota(angle_index[:], pattern=[[1, per_shape]], base=0, channel_multiplier=0, allow_small_or_imprecise_dtypes=True)
        for level in (0, 1):
            extra = keep.tile([P, ANCHORS, 3], F32, name="extra%d" % level)
            for i, wh in enumerate(LEVELS[level]["shapes"]):
                for f in range(2):
                    nc.vector.tensor_scalar(
                        out=extra[:, i * per_shape : (i + 1) * per_shape, f : f + 1], in0=zero[:].unsqueeze(2),
                        scalar1=1.0, scalar2=math.log(wh[f]), op0=ALU.mult, op1=ALU.add,
                    )
                nc.vector.tensor_scalar(
                    out=extra[:, i * per_shape : (i + 1) * per_shape, 2:3], in0=angle_index[:].unsqueeze(2),
                    scalar1=RADIANS_PER_DEGREE * (ANGLE_DEGREES[1] - ANGLE_DEGREES[0]), scalar2=RADIANS_PER_DEGREE * ANGLE_DEGREES[0],
                    op0=ALU.mult, op1=ALU.add,
                )
            tiles[level]["extra"] = extra

        def cell_centres(level):
            lv = LEVELS[level]
            grid = lv["grid"]
            groups = grid * grid // ROWS
            spot = tiles[level]["spot"]
            gx = keep.tile([P, groups], I32, name="gx%d" % level)
            nc.vector.tensor_scalar(out=gx[:], in0=spot[:], scalar1=grid - 1, scalar2=None, op0=ALU.bitwise_and)
            gy = keep.tile([P, groups], I32, name="gy%d" % level)
            nc.vector.tensor_scalar(
                out=gy[:], in0=spot[:], scalar1=grid * grid - 1, scalar2=lv["grid_bits"],
                op0=ALU.bitwise_and, op1=ALU.logical_shift_right,
            )
            centres = keep.tile([P, groups, 2], F32, name="centres%d" % level)
            for f, g in enumerate((gx, gy)):
                nc.vector.tensor_scalar(
                    out=centres[:, :, f : f + 1], in0=g[:].unsqueeze(2), scalar1=0.5, scalar2=lv["stride"],
                    op0=ALU.add, op1=ALU.mult,
                )
            tiles[level]["centres"] = centres

        def spread_bias(level):
            bias = keep.tile([P, OUT_CH], F32, name="bias%d" % level, align_bytes=256)
            for c0 in range(0, OUT_CH, BANK):
                width = min(BANK, OUT_CH - c0)
                spread = psum.tile([P, BANK], F32, tag="bank")
                nc.tensor.matmul(
                    out=spread[:, 0:width], lhsT=ones[:], rhs=bias_rows[:, level, c0 : c0 + width], start=True, stop=True
                )
                nc.scalar.copy(out=bias[:, c0 : c0 + width], in_=spread[:, 0:width])
            tiles[level]["bias"] = bias

        def times_one(out, in_):
            nc.gpsimd.tensor_scalar(out=out, in0=in_, scalar1=1.0, scalar2=0.0, op0=ALU.mult, op1=ALU.add)

        def regroup(level, copy):
            t = tiles[level]
            groups = LEVELS[level]["grid"] ** 2 // ROWS
            x_grouped = keep.tile([P, groups, P, PACK], BF16, name="x_grouped%d" % level, align_bytes=256)
            dst = x_grouped[:].rearrange("p j (b r) t -> p b r j t", r=ROWS)
            src = t["x_raw"][:].rearrange("p b (t r j) -> p b r j t", t=PACK, r=ROWS)
            images = LEVELS[level]["images_per_load"]
            few = min(groups, PACK)
            for first in range(0, BATCH, images):
                for j0 in range(0, groups, few):
                    copy(
                        out=dst[:, first : first + images, :, j0 : j0 + few, :],
                        in_=src[:, first : first + images, :, j0 : j0 + few, :],
                    )
            t["x_grouped"] = x_grouped

        def shift_bias(engine, level, a0, a1):
            t = tiles[level]
            part = t["bias"][:].rearrange("p (a f) -> p a f", f=FIELDS)[:, a0:a1, 2:5]
            engine.tensor_tensor(out=part, in0=part, in1=t["extra"][:, a0:a1], op=ALU.add)

        def quantise(level):
            t = tiles[level]
            groups = LEVELS[level]["grid"] ** 2 // ROWS
            x_grouped = t["x_grouped"]
            x_codes = keep.tile([P, groups * P], I32, name="x_codes%d" % level, align_bytes=256)
            x_plane = keep.tile([P, groups * P], U8, name="x_plane%d" % level, align_bytes=256)
            flat = x_grouped[:].rearrange("p j m t -> p (j m t)")
            step = min(QUANT_COLS, groups * P * PACK) // PACK
            for c0 in range(0, groups * P, step):
                nc.vector.quantize_mx(
                    out=x_codes[:, c0 : c0 + step].bitcast(FP8X4),
                    scales=x_plane[:, c0 : c0 + step],
                    in_=flat[:, PACK * c0 : PACK * (c0 + step)],
                )
                if level == 0 and c0 == 0:
                    shift_bias(nc.vector, 0, 0, FIRST_ANCHORS)
            t["x_codes"], t["x_plane"] = x_codes, x_plane
            t["res"] = keep.tile([P, ANCHORS, groups, FIELDS], F32, name="res%d" % level, align_bytes=256)

        def logits(level, a0, step):
            t = tiles[level]
            groups = LEVELS[level]["grid"] ** 2 // ROWS
            in_bank = min(groups, BANK // P)
            for a in range(a0, a0 + step, PAIR):
                cols = slice(a * FIELDS, (a + PAIR) * FIELDS)
                bias_pair = t["bias"][:, cols].rearrange("p (a f) -> p a f", f=FIELDS)
                for j0 in range(0, groups, in_bank):
                    bank = psum.tile([P, in_bank, P], F32, tag="bank")
                    for g in range(in_bank):
                        spots = slice((j0 + g) * P, (j0 + g + 1) * P)
                        nc.tensor.matmul_mx(
                            out=bank[:, g, :],
                            lhsT=t["x_codes"][:, spots].bitcast(FP8X4),
                            lhsT_scale=t["x_plane"][:, spots],
                            rhs=t["w_codes"][:, cols].bitcast(FP8X4),
                            rhs_scale=t["w_plane"][:, cols],
                            start=True,
                            stop=True,
                        )
                    nc.vector.tensor_tensor(
                        out=t["res"][:, a : a + PAIR, j0 : j0 + in_bank, :].rearrange("p a g f -> p g a f"),
                        in0=bank[:].rearrange("p g (a f) -> p g a f", f=FIELDS),
                        in1=bias_pair.unsqueeze(1).to_broadcast([P, in_bank, PAIR, FIELDS]),
                        op=ALU.add,
                    )

        def halve(engine, level, a0, step, first, last):
            part = tiles[level]["res"][:, a0 : a0 + step, :, first:last]
            engine.tensor_scalar(out=part, in0=part, scalar1=0.5, scalar2=0.5, op0=ALU.mult, op1=ALU.add)

        def activate_boxes(level, a0, step):
            part = tiles[level]["res"][:, a0 : a0 + step]
            nc.scalar.activation(out=part[:, :, :, 2:4], in_=part[:, :, :, 2:4], func=ACT.Exp)
            nc.scalar.activation(out=part[:, :, :, 0:2], in_=part[:, :, :, 0:2], func=ACT.Tanh, scale=0.5)

        def activate_sigmoids(level, a0, step):
            part = tiles[level]["res"][:, a0 : a0 + step, :, 5:FIELDS]
            nc.scalar.activation(out=part, in_=part, func=ACT.Tanh, scale=0.5)

        def finish_boxes(level, a0, step):
            lv = LEVELS[level]
            t = tiles[level]
            groups = lv["grid"] ** 2 // ROWS
            part = t["res"][:, a0 : a0 + step]
            nc.vector.scalar_tensor_tensor(
                out=part[:, :, :, 0:2],
                in0=part[:, :, :, 0:2],
                scalar=lv["sxy"] * lv["stride"] / 2.0,
                in1=t["centres"][:].unsqueeze(1).to_broadcast([P, step, groups, 2]),
                op0=ALU.mult,
                op1=ALU.add,
            )

        def store(level, a0, step):
            lv = LEVELS[level]
            t = tiles[level]
            spots = lv["grid"] ** 2
            for a in range(a0, a0 + step):
                row = lv["first_row"] + a * spots
                nc.sync.dma_start(
                    out=out[:, row : row + spots, :].rearrange("b (r j) f -> b r (j f)", r=ROWS),
                    in_=t["res"][:, a].rearrange("p j f -> p (j f)"),
                )

        for level in (0, 1):
            spread_bias(level)
            cell_centres(level)
        regroup(1, times_one)
        shift_bias(nc.gpsimd, 1, 0, ANCHORS)
        regroup(0, nc.vector.tensor_copy)
        quantise(0)

        chunks = []
        for level in (0, 1):
            step = PAIR * LEVELS[level]["pairs"]
            chunks.extend((level, a0, step) for a0 in range(0, ANCHORS, step))
        large = ANCHORS // PAIR
        chunks = chunks[0:SMALL_LEVEL_AT] + chunks[large:] + chunks[SMALL_LEVEL_AT:large]

        def finish(level, a0, step):
            halve(nc.vector, level, a0, step, 5, HEAD)
            finish_boxes(level, a0, step)
            store(level, a0, step)

        last = len(chunks) - 1
        for i, chunk in enumerate(chunks):
            logits(*chunk)
            if i == 0:
                shift_bias(nc.vector, 0, FIRST_ANCHORS, ANCHORS)
            if i < last:
                activate_sigmoids(*chunk)
                halve(nc.gpsimd, *chunk, HEAD, FIELDS)
                activate_boxes(*chunk)
            if i == PREPARE_AT:
                quantise(1)
            if i >= LAG:
                finish(*chunks[i - LAG])
        finish(*chunks[last - 1])
        level, a0, step = chunks[last]
        activate_boxes(level, a0, step)
        for a in range(a0, a0 + step):
            activate_sigmoids(level, a, 1)
        finish_boxes(level, a0, step)
        for a in range(a0, a0 + step):
            halve(nc.vector, level, a, 1, 5, FIELDS)
            store(level, a, 1)
